import numpy as np
import ml_dtypes


def mxq(x, axis, fmt="e4m3"):
    dtype, down = {"e4m3": (ml_dtypes.float8_e4m3fn, 7), "e5m2": (ml_dtypes.float8_e5m2, 14)}[fmt]
    v = np.moveaxis(np.asarray(x, np.float32).astype(ml_dtypes.bfloat16).astype(np.float64), axis, -1)
    blocks = v.reshape(v.shape[:-1] + (-1, 32))
    amax = np.abs(blocks).max(-1, keepdims=True)
    byte = np.maximum(np.where(amax > 0, np.frexp(amax)[1] - 1 + 127, 0) - down, 1)
    scale = np.exp2(byte - 127.0)
    codes = (blocks / scale).astype(np.float32).astype(dtype).astype(np.float64)
    return np.moveaxis((codes * scale).reshape(v.shape), -1, axis)


WIDE = False


def mx_kscale(k):
    if not WIDE:
        return np.ones(k)
    levels = np.array([10, -10, 5, -5, 0])
    a = np.random.permutation(np.resize(levels, k // 512 * 4)).reshape(k // 512, 4)
    idx = np.arange(k)
    return np.exp2(a[idx // 512, idx % 128 // 32])


BF16 = ml_dtypes.bfloat16


def bf(x):
    return np.asarray(x, np.float32).astype(BF16)


def f64(x):
    return np.asarray(x).astype(np.float64)


B, S, E, H, D = 2, 512, 512, 4, 512


def setup_inputs():
    s = mx_kscale(E)
    ckv = 0.75 * D ** 0.25 / np.sqrt(E)
    cq = 3.0 / np.sqrt(E)
    return {"x": bf(np.random.standard_normal((B, S, E)) * s),
            "Wq": bf(np.random.standard_normal((E, H * D)) * cq / s[:, None]),
            "bq": bf(np.random.standard_normal(H * D) * 0.25),
            "Wk": bf(np.random.standard_normal((E, H * D)) * ckv / s[:, None]),
            "bk": bf(np.random.standard_normal(H * D)),
            "Wv": bf(np.random.standard_normal((E, H * D)) * ckv / s[:, None]),
            "bv": bf(np.random.standard_normal(H * D))}


def reference(x, Wq, bq, Wk, bk, Wv, bv):
    xq = mxq(f64(x), 2, "e4m3")

    def proj(W, bias):
        y = (xq @ mxq(f64(W), 0, "e4m3")) + f64(bias)
        return y.reshape(B, S, H, D).transpose(0, 2, 1, 3)

    q = proj(Wq, bq)
    k = proj(Wk, bk)
    v = proj(Wv, bv)
    kv = k * np.swapaxes(v, -1, -2) * (1.0 / np.sqrt(D))
    e = np.exp(kv - kv.max(axis=2, keepdims=True))
    attn = e / e.sum(axis=2, keepdims=True)
    return np.sum(attn * q, axis=2)

@@ -1,0 +1,324 @@
+from contextlib import ExitStack
+import math
+
+import concourse.masks as masks
+import concourse.mybir as mybir
+
+BF16 = mybir.dt.bfloat16
+F32 = mybir.dt.float32
+U32 = mybir.dt.uint32
+U8 = mybir.dt.uint8
+FP8X4 = mybir.dt.float8_e4m3fn_x4
+ALU = mybir.AluOpType
+ACT = mybir.ActivationFunctionType
+
+P = 128
+PACK = 4
+B, S, E, H, D = 2, 512, 512, 4, 512
+assert E == P * PACK and S == D
+
+J_TILES = D // P
+TILES_PER_HEAD = B * J_TILES
+N_TILES = H * TILES_PER_HEAD
+TOKEN_TILES = S // P
+HALF_E = E // 2
+
+RUN = 4
+PIECE_COLS = 64
+PIECES = D // PIECE_COLS
+PIECES_PER_PERIOD = 3
+
+FLOPS = 2 * B * S * E * 3 * H * D
+
+
+def tile_multihead_attention_pa_kernel(tc, x, Wq, bq, Wk, bk, Wv, bv, out):
+    nc = tc.nc
+    weights = {"q": Wq, "k": Wk, "v": Wv}
+    score_scale = 1.0 / math.sqrt(D)
+
+    with ExitStack() as ctx:
+        keep = ctx.enter_context(tc.tile_pool(name="keep", bufs=1))
+        group_pool = ctx.enter_context(tc.tile_pool(name="group", bufs=3))
+        work = ctx.enter_context(tc.tile_pool(name="work", bufs=2))
+        psum = ctx.enter_context(tc.psum_pool(name="psum", bufs=2))
+        ctx.enter_context(tc.manual_schedule())
+
+        x_raw = keep.tile([P, B * TOKEN_TILES * E], BF16)
+        x_grouped = keep.tile([P, B * S * PACK], BF16, align_bytes=64)
+        x_codes = keep.tile([P, B * S], U32, align_bytes=64)
+        x_scales = keep.tile([P, B * S], U8, align_bytes=64)
+        codes = {}
+        scales = {}
+        for which in ("k", "v", "q"):
+            codes[which] = keep.tile([P, H * D], U32, name="codes_" + which, align_bytes=64)
+            scales[which] = keep.tile([P, H * D], U8, name="scales_" + which, align_bytes=64)
+        raw_blocks = {}
+
+        identity = keep.tile([P, P], F32)
+        bias_stage = keep.tile([2 * H * J_TILES, P], BF16)
+        bias_rows = keep.tile([P, P], F32)
+        neg_bk = keep.tile([P, H * J_TILES], F32)
+        bq_cols = keep.tile([P, H * J_TILES], F32)
+        bv_all = keep.tile([P, H * D], BF16)
+        zero_col = keep.tile([P, 1], F32)
+        table_warm = keep.tile([P, 1], F32)
+        neg_max = keep.tile([P, N_TILES], F32)
+        denominator = keep.tile([P, N_TILES], F32)
+        numerator = keep.tile([P, N_TILES], F32)
+        reciprocal = keep.tile([P, N_TILES], F32)
+        result = keep.tile([P, P], F32)
+        result_rows = keep.tile([N_TILES, P], F32)
+        products = keep.tile([P, S], F32)
+
+        def load_x(batch):
+            first = batch * TOKEN_TILES * E
+            nc.sync.dma_start(
+                out=x_raw[:, first : first + TOKEN_TILES * E].rearrange("p (n e) -> p n e", e=E),
+                in_=x[batch].rearrange("(n p) e -> p n e", p=P),
+            )
+
+        def load_weight_block(which, head):
+            raw = keep.tile([P, PACK, D], BF16, name="raw_%s%d" % (which, head))
+            for half in range(2):
+                rows = weights[which][half * HALF_E : (half + 1) * HALF_E, head * D : (head + 1) * D]
+                nc.sync.dma_start(
+                    out=raw[:, 2 * half : 2 * half + 2, :], in_=rows.rearrange("(p e) c -> p e c", e=2)
+                )
+            raw_blocks[(which, head)] = raw
+
+        load_x(0)
+        load_weight_block("v", 0)
+        load_weight_block("k", 0)
+        load_weight_block("q", 0)
+        load_x(1)
+        for head in range(1, H):
+            for which in ("k", "v", "q"):
+                load_weight_block(which, head)
+
+        n_bias_rows = H * J_TILES
+        nc.scalar.dma_start(out=bias_stage[0:n_bias_rows, :], in_=bk.rearrange("(r p) -> r p", p=P))
+        nc.scalar.dma_start(out=bias_stage[n_bias_rows : 2 * n_bias_rows, :], in_=bq.rearrange("(r p) -> r p", p=P))
+        nc.scalar.dma_start(out=bv_all[:], in_=bv.partition_broadcast(P))
+
+        masks.make_identity(nc, identity[:])
+        nc.vector.memset(zero_col[:], 0.0)
+        nc.vector.memset(bias_rows[:], 0.0)
+        nc.vector.memset(result[:], 0.0)
+        nc.scalar.activation(out=table_warm[:], in_=zero_col[:], func=ACT.Exp)
+
+        nc.vector.tensor_copy(out=bias_rows[0 : 2 * n_bias_rows, :], in_=bias_stage[:])
+        bias_cols = psum.tile([P, P], F32, tag="misc")
+        nc.tensor.transpose(bias_cols[:], bias_rows[:], identity[:])
+        nc.vector.tensor_scalar_mul(out=neg_bk[:], in0=bias_cols[:, 0:n_bias_rows], scalar1=-score_scale)
+        nc.vector.tensor_copy(out=bq_cols[:], in_=bias_cols[:, n_bias_rows : 2 * n_bias_rows])
+
+        def quantise(grouped, codes_out, scales_out):
+            nc.vector.quantize_mx(out=codes_out.bitcast(FP8X4), scales=scales_out, in_=grouped)
+
+        def x_job(batch):
+            return (
+                x_grouped[:, batch * S * PACK : (batch + 1) * S * PACK],
+                x_codes[:, batch * S : (batch + 1) * S],
+                x_scales[:, batch * S : (batch + 1) * S],
+            )
+
+        def weight_job(grouped, which, head):
+            cols = slice(head * D, (head + 1) * D)
+            return (grouped[:].rearrange("p c t -> p (c t)"), codes[which][:, cols], scales[which][:, cols])
+
+        def transpose_x(batch):
+            x_words = x_raw[:].bitcast(F32)
+            grouped_words = x_grouped[:].bitcast(F32)
+            for pair in range(TOKEN_TILES // 2):
+                turned = psum.tile([P, 2, 2 * P], F32, tag="misc")
+                for block in range(2):
+                    n = batch * TOKEN_TILES + 2 * pair + block
+                    for half in range(2):
+                        first = n * (E // 2) + half * P
+                        nc.tensor.transpose(
+                            turned[:, half, block * P : (block + 1) * P], x_words[:, first : first + P], identity[:]
+                        )
+                first_token = batch * S + pair * 2 * P
+                nc.scalar.copy(
+                    out=grouped_words[:, 2 * first_token : 2 * (first_token + 2 * P)].rearrange(
+                        "p (r u) -> p r u", u=2
+                    ),
+                    in_=turned[:].rearrange("p u r -> p r u"),
+                )
+
+        def regroup(copy, raw, grouped, first_col, n_cols):
+            cols = slice(first_col, first_col + n_cols)
+            copy(
+                out=grouped[:, cols, :].rearrange("p (c i) t -> p c t i", i=RUN),
+                in_=raw[:, :, cols].rearrange("p t (c i) -> p c t i", i=RUN),
+            )
+
+        def new_grouped():
+            grouped = group_pool.tile([P, D, PACK], BF16, name="grouped", align_bytes=64)
+            return grouped
+
+        to_quantise = {n: [] for n in range(-1, N_TILES + 4)}
+
+        stream = [(which, head) for head in range(1, H) for which in ("k", "v", "q")]
+        stream_grouped = {}
+
+        def regroup_stream_piece(n, period):
+            if n >= len(stream) * PIECES:
+                return
+            block, piece = divmod(n, PIECES)
+            which, head = stream[block]
+            if piece == 0:
+                stream_grouped[block] = new_grouped()
+            regroup(nc.scalar.copy, raw_blocks[(which, head)], stream_grouped[block], piece * PIECE_COLS, PIECE_COLS)
+            if piece == PIECES - 1:
+                to_quantise[period + 1].append(weight_job(stream_grouped[block], which, head))
+
+        live = {}
+
+        def place(t):
+            head, rest = divmod(t, TILES_PER_HEAD)
+            batch, j_tile = divmod(rest, J_TILES)
+            return head, batch, j_tile
+
+        def out_row(t):
+            head, batch, j_tile = place(t)
+            return (batch * H + head) * J_TILES + j_tile
+
+        def project(name, t, stationary, stationary_cols, moving, moving_cols):
+            bank = psum.tile([P, S], F32, name=name + "_ps", tag=name)
+            nc.tensor.matmul_mx(
+                out=bank[:],
+                lhsT=stationary[0][:, stationary_cols].bitcast(FP8X4),
+                lhsT_scale=stationary[1][:, stationary_cols],
+                rhs=moving[0][:, moving_cols].bitcast(FP8X4),
+                rhs_scale=moving[1][:, moving_cols],
+                start=True,
+                stop=True,
+            )
+            live[(name, t)] = bank
+
+        def feature_cols(t):
+            head, batch, j_tile = place(t)
+            return slice(head * D + j_tile * P, head * D + (j_tile + 1) * P)
+
+        def project_k_and_v(t):
+            if not 0 <= t < N_TILES:
+                return
+            head, batch, j_tile = place(t)
+            all_tokens = slice(batch * S, (batch + 1) * S)
+            my_tokens = slice(batch * S + j_tile * P, batch * S + (j_tile + 1) * P)
+            project("k", t, (codes["k"], scales["k"]), feature_cols(t), (x_codes, x_scales), all_tokens)
+            project("v", t, (x_codes, x_scales), my_tokens, (codes["v"], scales["v"]), slice(head * D, (head + 1) * D))
+
+        def project_q(t):
+            if not 0 <= t < N_TILES:
+                return
+            head, batch, j_tile = place(t)
+            all_tokens = slice(batch * S, (batch + 1) * S)
+            project("q", t, (codes["q"], scales["q"]), feature_cols(t), (x_codes, x_scales), all_tokens)
+
+        def add_biases(t):
+            if not 0 <= t < N_TILES:
+                return
+            head, batch, j_tile = place(t)
+            bias_col = head * J_TILES + j_tile
+            neg_k = work.tile([P, S], F32, name="neg_k")
+            nc.scalar.activation(
+                out=neg_k[:],
+                in_=live[("k", t)][:],
+                func=ACT.Identity,
+                bias=neg_bk[:, bias_col : bias_col + 1],
+                scale=-score_scale,
+            )
+            v_full = work.tile([P, S], F32, name="v_full")
+            nc.vector.tensor_tensor(
+                out=v_full[:], in0=live[("v", t)][:], in1=bv_all[:, head * D : (head + 1) * D], op=ALU.add
+            )
+            live[("neg_k", t)] = neg_k
+            live[("v_full", t)] = v_full
+
+        def multiply_scores(t):
+            if not 0 <= t < N_TILES:
+                return
+            neg_score = work.tile([P, S], F32, name="neg_score", bufs=3)
+            nc.gpsimd.tensor_tensor(out=neg_score[:], in0=live[("neg_k", t)][:], in1=live[("v_full", t)][:], op=ALU.mult)
+            live[("neg_score", t)] = neg_score
+
+        def row_maximum(t):
+            if not 0 <= t < N_TILES:
+                return
+            col = out_row(t)
+            nc.vector.tensor_reduce(
+                out=neg_max[:, col : col + 1], in_=live[("neg_score", t)][:], axis=mybir.AxisListType.X, op=ALU.min
+            )
+
+        def exponentials(t):
+            if not 0 <= t < N_TILES:
+                return
+            col = out_row(t)
+            weight = work.tile([P, S], F32, name="weight")
+            nc.scalar.activation(
+                out=weight[:],
+                in_=live[("neg_score", t)][:],
+                func=ACT.Exp,
+                bias=neg_max[:, col : col + 1],
+                scale=-1.0,
+                accum_out=denominator[:, col : col + 1],
+            )
+            live[("weight", t)] = weight
+
+        def weighted_sum(t):
+            if not 0 <= t < N_TILES:
+                return
+            col = out_row(t)
+            nc.vector.scalar_tensor_tensor(
+                out=products[:],
+                in0=live[("q", t)][:],
+                scalar=1.0,
+                in1=live[("weight", t)][:],
+                op0=ALU.mult,
+                op1=ALU.mult,
+                accum_out=numerator[:, col : col + 1],
+            )
+
+        transpose_x(0)
+        first_grouped = {}
+        for which in ("v", "k"):
+            first_grouped[which] = new_grouped()
+            regroup(nc.vector.tensor_copy, raw_blocks[(which, 0)], first_grouped[which], 0, D)
+        quantise(*x_job(0))
+        for which in ("v", "k"):
+            quantise(*weight_job(first_grouped[which], which, 0))
+
+        for period in range(-1, N_TILES + 2):
+            project_q(period - 2)
+            project_k_and_v(period + 1)
+            add_biases(period)
+            multiply_scores(period)
+            if period == 0:
+                first_grouped["q"] = new_grouped()
+                regroup(nc.vector.tensor_copy, raw_blocks[("q", 0)], first_grouped["q"], 0, D)
+                to_quantise[period + 1].append(weight_job(first_grouped["q"], "q", 0))
+                transpose_x(1)
+                to_quantise[period + 1].append(x_job(1))
+            if period >= 0:
+                for n in range(PIECES_PER_PERIOD):
+                    regroup_stream_piece(period * PIECES_PER_PERIOD + n, period)
+            row_maximum(period - 1)
+            exponentials(period - 1)
+            weighted_sum(period - 2)
+            for job in to_quantise[period]:
+                quantise(*job)
+
+        nc.vector.reciprocal(out=reciprocal[:], in_=denominator[:])
+        nc.vector.tensor_tensor(out=result[:, 0:N_TILES], in0=numerator[:], in1=reciprocal[:], op=ALU.mult)
+        nc.vector.tensor_tensor(
+            out=result[:, 0:N_TILES].rearrange("p (b r) -> p b r", b=B),
+            in0=result[:, 0:N_TILES].rearrange("p (b r) -> p b r", b=B),
+            in1=bq_cols[:].unsqueeze(1).to_broadcast([P, B, n_bias_rows]),
+            op=ALU.add,
+        )
+        turned_result = psum.tile([P, P], F32, tag="misc")
+        nc.tensor.transpose(turned_result[:], result[:], identity[:])
+        nc.scalar.copy(out=result_rows[:], in_=turned_result[0:N_TILES, :])
+        nc.sync.dma_start(out=out.rearrange("b h (n p) -> (b h n) p", p=P), in_=result_rows[:])

@@ -39,7 +39,7 @@ def tile_multihead_attention_pa_kernel(tc, x, Wq, bq, Wk, bk, Wv, bv, out):
     with ExitStack() as ctx:
         keep = ctx.enter_context(tc.tile_pool(name="keep", bufs=1))
         group_pool = ctx.enter_context(tc.tile_pool(name="group", bufs=3))
-        work = ctx.enter_context(tc.tile_pool(name="work", bufs=2))
+        work = ctx.enter_context(tc.tile_pool(name="work", bufs=3))
         psum = ctx.enter_context(tc.psum_pool(name="psum", bufs=2))
         ctx.enter_context(tc.manual_schedule())
 
@@ -157,7 +157,7 @@ def tile_multihead_attention_pa_kernel(tc, x, Wq, bq, Wk, bk, Wv, bv, out):
             grouped = group_pool.tile([P, D, PACK], BF16, name="grouped", align_bytes=64)
             return grouped
 
-        to_quantise = {n: [] for n in range(-1, N_TILES + 4)}
+        to_quantise = {n: [] for n in range(-1, N_TILES + 6)}
 
         stream = [(which, head) for head in range(1, H) for which in ("k", "v", "q")]
         stream_grouped = {}
@@ -240,7 +240,7 @@ def tile_multihead_attention_pa_kernel(tc, x, Wq, bq, Wk, bk, Wv, bv, out):
         def multiply_scores(t):
             if not 0 <= t < N_TILES:
                 return
-            neg_score = work.tile([P, S], F32, name="neg_score", bufs=3)
+            neg_score = work.tile([P, S], F32, name="neg_score", bufs=5)
             nc.gpsimd.tensor_tensor(out=neg_score[:], in0=live[("neg_k", t)][:], in1=live[("v_full", t)][:], op=ALU.mult)
             live[("neg_score", t)] = neg_score
 
@@ -290,8 +290,8 @@ def tile_multihead_attention_pa_kernel(tc, x, Wq, bq, Wk, bk, Wv, bv, out):
         for which in ("v", "k"):
             quantise(*weight_job(first_grouped[which], which, 0))
 
-        for period in range(-1, N_TILES + 2):
-            project_q(period - 2)
+        for period in range(-1, N_TILES + 4):
+            project_q(period - 3)
             project_k_and_v(period + 1)
             add_biases(period)
             multiply_scores(period)
@@ -304,9 +304,9 @@ def tile_multihead_attention_pa_kernel(tc, x, Wq, bq, Wk, bk, Wv, bv, out):
             if period >= 0:
                 for n in range(PIECES_PER_PERIOD):
                     regroup_stream_piece(period * PIECES_PER_PERIOD + n, period)
-            row_maximum(period - 1)
-            exponentials(period - 1)
-            weighted_sum(period - 2)
+            row_maximum(period - 2)
+            exponentials(period - 3)
+            weighted_sum(period - 4)
             for job in to_quantise[period]:
                 quantise(*job)
 

@@ -23,10 +23,18 @@ N_TILES = H * TILES_PER_HEAD
 TOKEN_TILES = S // P
 HALF_E = E // 2
 
+BLOCKS = ("k", "v", "q")
+BLOCK_COL = {"k": 0, "v": D, "q": 2 * D}
+HEAD_COLS = 3 * D
+HALF_D = D // 2
+
 RUN = 4
+STEP_COLS = HEAD_COLS // TILES_PER_HEAD
 PIECE_COLS = 64
-PIECES = D // PIECE_COLS
-PIECES_PER_PERIOD = 3
+
+MAX_LAG = 2
+EXP_LAG = 3
+SUM_LAG = 4
 
 FLOPS = 2 * B * S * E * 3 * H * D
 
@@ -35,10 +43,11 @@ def tile_multihead_attention_pa_kernel(tc, x, Wq, bq, Wk, bk, Wv, bv, out):
     nc = tc.nc
     weights = {"q": Wq, "k": Wk, "v": Wv}
     score_scale = 1.0 / math.sqrt(D)
+    n_bias_rows = H * J_TILES
 
     with ExitStack() as ctx:
         keep = ctx.enter_context(tc.tile_pool(name="keep", bufs=1))
-        group_pool = ctx.enter_context(tc.tile_pool(name="group", bufs=3))
+        group_pool = ctx.enter_context(tc.tile_pool(name="group", bufs=2))
         work = ctx.enter_context(tc.tile_pool(name="work", bufs=3))
         psum = ctx.enter_context(tc.psum_pool(name="psum", bufs=2))
         ctx.enter_context(tc.manual_schedule())
@@ -47,18 +56,23 @@ def tile_multihead_attention_pa_kernel(tc, x, Wq, bq, Wk, bk, Wv, bv, out):
         x_grouped = keep.tile([P, B * S * PACK], BF16, align_bytes=64)
         x_codes = keep.tile([P, B * S], U32, align_bytes=64)
         x_scales = keep.tile([P, B * S], U8, align_bytes=64)
+        raw = {}
         codes = {}
         scales = {}
-        for which in ("k", "v", "q"):
-            codes[which] = keep.tile([P, H * D], U32, name="codes_" + which, align_bytes=64)
-            scales[which] = keep.tile([P, H * D], U8, name="scales_" + which, align_bytes=64)
-        raw_blocks = {}
+        grouped = {}
+        for head in range(H):
+            for which in BLOCKS:
+                raw[(which, head)] = keep.tile([P, PACK, D], BF16, name="raw_%s%d" % (which, head))
+            codes[head] = keep.tile([P, HEAD_COLS], U32, name="codes%d" % head, align_bytes=64)
+            scales[head] = keep.tile([P, HEAD_COLS], U8, name="scales%d" % head, align_bytes=64)
 
         identity = keep.tile([P, P], F32)
-        bias_stage = keep.tile([2 * H * J_TILES, P], BF16)
-        bias_rows = keep.tile([P, P], F32)
-        neg_bk = keep.tile([P, H * J_TILES], F32)
-        bq_cols = keep.tile([P, H * J_TILES], F32)
+        identity_bf = keep.tile([P, P], BF16)
+        n_stage_rows = 2 * n_bias_rows + J_TILES
+        bias_rows = keep.tile([P, P], BF16)
+        neg_bk = keep.tile([P, n_bias_rows], F32)
+        bq_cols = keep.tile([P, n_bias_rows], F32)
+        bv0_cols = keep.tile([P, J_TILES], BF16)
         bv_all = keep.tile([P, H * D], BF16)
         zero_col = keep.tile([P, 1], F32)
         table_warm = keep.tile([P, 1], F32)
@@ -78,42 +92,44 @@ def tile_multihead_attention_pa_kernel(tc, x, Wq, bq, Wk, bk, Wv, bv, out):
             )
 
         def load_weight_block(which, head):
-            raw = keep.tile([P, PACK, D], BF16, name="raw_%s%d" % (which, head))
             for half in range(2):
                 rows = weights[which][half * HALF_E : (half + 1) * HALF_E, head * D : (head + 1) * D]
                 nc.sync.dma_start(
-                    out=raw[:, 2 * half : 2 * half + 2, :], in_=rows.rearrange("(p e) c -> p e c", e=2)
+                    out=raw[(which, head)][:, 2 * half : 2 * half + 2, :],
+                    in_=rows.rearrange("(p e) c -> p e c", e=2),
                 )
-            raw_blocks[(which, head)] = raw
 
-        load_x(0)
+        def load_bv(head):
+            cols = slice(head * D, (head + 1) * D)
+            nc.sync.dma_start(out=bv_all[:, cols], in_=bv[cols].partition_broadcast(P))
+
         load_weight_block("v", 0)
+        load_x(0)
         load_weight_block("k", 0)
         load_weight_block("q", 0)
+        load_weight_block("k", 1)
         load_x(1)
-        for head in range(1, H):
+        load_weight_block("v", 1)
+        load_weight_block("q", 1)
+        load_bv(1)
+        for head in range(2, H):
             for which in ("k", "v", "q"):
                 load_weight_block(which, head)
+            load_bv(head)
 
-        n_bias_rows = H * J_TILES
-        nc.scalar.dma_start(out=bias_stage[0:n_bias_rows, :], in_=bk.rearrange("(r p) -> r p", p=P))
-        nc.scalar.dma_start(out=bias_stage[n_bias_rows : 2 * n_bias_rows, :], in_=bq.rearrange("(r p) -> r p", p=P))
-        nc.scalar.dma_start(out=bv_all[:], in_=bv.partition_broadcast(P))
+        nc.vector.memset(bias_rows[:], 0.0)
+        nc.scalar.dma_start(out=bias_rows[0:n_bias_rows, :], in_=bk.rearrange("(r p) -> r p", p=P))
+        nc.scalar.dma_start(out=bias_rows[n_bias_rows : 2 * n_bias_rows, :], in_=bq.rearrange("(r p) -> r p", p=P))
+        nc.scalar.dma_start(out=bias_rows[2 * n_bias_rows : n_stage_rows, :], in_=bv[0:D].rearrange("(r p) -> r p", p=P))
 
         masks.make_identity(nc, identity[:])
         nc.vector.memset(zero_col[:], 0.0)
-        nc.vector.memset(bias_rows[:], 0.0)
         nc.vector.memset(result[:], 0.0)
+        nc.vector.tensor_copy(out=identity_bf[:], in_=identity[:])
         nc.scalar.activation(out=table_warm[:], in_=zero_col[:], func=ACT.Exp)
 
-        nc.vector.tensor_copy(out=bias_rows[0 : 2 * n_bias_rows, :], in_=bias_stage[:])
-        bias_cols = psum.tile([P, P], F32, tag="misc")
-        nc.tensor.transpose(bias_cols[:], bias_rows[:], identity[:])
-        nc.vector.tensor_scalar_mul(out=neg_bk[:], in0=bias_cols[:, 0:n_bias_rows], scalar1=-score_scale)
-        nc.vector.tensor_copy(out=bq_cols[:], in_=bias_cols[:, n_bias_rows : 2 * n_bias_rows])
-
-        def quantise(grouped, codes_out, scales_out):
-            nc.vector.quantize_mx(out=codes_out.bitcast(FP8X4), scales=scales_out, in_=grouped)
+        def quantise(in_, codes_out, scales_out):
+            nc.vector.quantize_mx(out=codes_out.bitcast(FP8X4), scales=scales_out, in_=in_)
 
         def x_job(batch):
             return (
@@ -122,9 +138,9 @@ def tile_multihead_attention_pa_kernel(tc, x, Wq, bq, Wk, bk, Wv, bv, out):
                 x_scales[:, batch * S : (batch + 1) * S],
             )
 
-        def weight_job(grouped, which, head):
-            cols = slice(head * D, (head + 1) * D)
-            return (grouped[:].rearrange("p c t -> p (c t)"), codes[which][:, cols], scales[which][:, cols])
+        def weight_job(head, first_col, n_cols):
+            cols = slice(first_col, first_col + n_cols)
+            return (grouped[head][:, cols, :].rearrange("p c t -> p (c t)"), codes[head][:, cols], scales[head][:, cols])
 
         def transpose_x(batch):
             x_words = x_raw[:].bitcast(F32)
@@ -146,32 +162,33 @@ def tile_multihead_attention_pa_kernel(tc, x, Wq, bq, Wk, bk, Wv, bv, out):
                     in_=turned[:].rearrange("p u r -> p r u"),
                 )
 
-        def regroup(copy, raw, grouped, first_col, n_cols):
-            cols = slice(first_col, first_col + n_cols)
+        def new_grouped(head):
+            grouped[head] = group_pool.tile([P, HEAD_COLS, PACK], BF16, name="grouped", align_bytes=64)
+
+        def regroup(copy, head, first_col, n_cols):
+            block, first_in_block = divmod(first_col, D)
             copy(
-                out=grouped[:, cols, :].rearrange("p (c i) t -> p c t i", i=RUN),
-                in_=raw[:, :, cols].rearrange("p t (c i) -> p c t i", i=RUN),
+                out=grouped[head][:, first_col : first_col + n_cols, :].rearrange("p (c i) t -> p c t i", i=RUN),
+                in_=raw[(BLOCKS[block], head)][:, :, first_in_block : first_in_block + n_cols].rearrange(
+                    "p t (c i) -> p c t i", i=RUN
+                ),
             )
 
-        def new_grouped():
-            grouped = group_pool.tile([P, D, PACK], BF16, name="grouped", align_bytes=64)
-            return grouped
+        last_period = N_TILES + SUM_LAG
+        to_quantise = {n: [] for n in range(last_period)}
 
-        to_quantise = {n: [] for n in range(-1, N_TILES + 6)}
-
-        stream = [(which, head) for head in range(1, H) for which in ("k", "v", "q")]
-        stream_grouped = {}
-
-        def regroup_stream_piece(n, period):
-            if n >= len(stream) * PIECES:
+        def regroup_next_head(period):
+            if not 0 <= period < (H - 1) * TILES_PER_HEAD:
                 return
-            block, piece = divmod(n, PIECES)
-            which, head = stream[block]
-            if piece == 0:
-                stream_grouped[block] = new_grouped()
-            regroup(nc.scalar.copy, raw_blocks[(which, head)], stream_grouped[block], piece * PIECE_COLS, PIECE_COLS)
-            if piece == PIECES - 1:
-                to_quantise[period + 1].append(weight_job(stream_grouped[block], which, head))
+            head, step = divmod(period, TILES_PER_HEAD)
+            head += 1
+            if step == 0:
+                new_grouped(head)
+            for first_col in range(step * STEP_COLS, (step + 1) * STEP_COLS, PIECE_COLS):
+                regroup(nc.scalar.copy, head, first_col, PIECE_COLS)
+            for first_col, n_cols in ((BLOCK_COL["k"], 2 * D), (BLOCK_COL["q"], D)):
+                if step * STEP_COLS < first_col + n_cols <= (step + 1) * STEP_COLS:
+                    to_quantise[period + 1].append(weight_job(head, first_col, n_cols))
 
         live = {}
 
@@ -197,25 +214,29 @@ def tile_multihead_attention_pa_kernel(tc, x, Wq, bq, Wk, bk, Wv, bv, out):
             )
             live[(name, t)] = bank
 
-        def feature_cols(t):
+        def project_features(name, t):
             head, batch, j_tile = place(t)
-            return slice(head * D + j_tile * P, head * D + (j_tile + 1) * P)
+            first = BLOCK_COL[name] + j_tile * P
+            project(
+                name, t, (codes[head], scales[head]), slice(first, first + P),
+                (x_codes, x_scales), slice(batch * S, (batch + 1) * S),
+            )
 
         def project_k_and_v(t):
             if not 0 <= t < N_TILES:
                 return
             head, batch, j_tile = place(t)
-            all_tokens = slice(batch * S, (batch + 1) * S)
-            my_tokens = slice(batch * S + j_tile * P, batch * S + (j_tile + 1) * P)
-            project("k", t, (codes["k"], scales["k"]), feature_cols(t), (x_codes, x_scales), all_tokens)
-            project("v", t, (x_codes, x_scales), my_tokens, (codes["v"], scales["v"]), slice(head * D, (head + 1) * D))
+            project_features("k", t)
+            first = batch * S + j_tile * P
+            project(
+                "v", t, (x_codes, x_scales), slice(first, first + P),
+                (codes[head], scales[head]), slice(BLOCK_COL["v"], BLOCK_COL["v"] + D),
+            )
 
         def project_q(t):
             if not 0 <= t < N_TILES:
                 return
-            head, batch, j_tile = place(t)
-            all_tokens = slice(batch * S, (batch + 1) * S)
-            project("q", t, (codes["q"], scales["q"]), feature_cols(t), (x_codes, x_scales), all_tokens)
+            project_features("q", t)
 
         def add_biases(t):
             if not 0 <= t < N_TILES:
@@ -240,7 +261,7 @@ def tile_multihead_attention_pa_kernel(tc, x, Wq, bq, Wk, bk, Wv, bv, out):
         def multiply_scores(t):
             if not 0 <= t < N_TILES:
                 return
-            neg_score = work.tile([P, S], F32, name="neg_score", bufs=5)
+            neg_score = work.tile([P, S], F32, name="neg_score", bufs=EXP_LAG + 2)
             nc.gpsimd.tensor_tensor(out=neg_score[:], in0=live[("neg_k", t)][:], in1=live[("v_full", t)][:], op=ALU.mult)
             live[("neg_score", t)] = neg_score
 
@@ -270,54 +291,64 @@ def tile_multihead_attention_pa_kernel(tc, x, Wq, bq, Wk, bk, Wv, bv, out):
         def weighted_sum(t):
             if not 0 <= t < N_TILES:
                 return
+            head, batch, j_tile = place(t)
+            bias_col = head * J_TILES + j_tile
             col = out_row(t)
             nc.vector.scalar_tensor_tensor(
                 out=products[:],
                 in0=live[("q", t)][:],
-                scalar=1.0,
+                scalar=bq_cols[:, bias_col : bias_col + 1],
                 in1=live[("weight", t)][:],
-                op0=ALU.mult,
+                op0=ALU.add,
                 op1=ALU.mult,
                 accum_out=numerator[:, col : col + 1],
             )
 
         transpose_x(0)
-        first_grouped = {}
-        for which in ("v", "k"):
-            first_grouped[which] = new_grouped()
-            regroup(nc.vector.tensor_copy, raw_blocks[(which, 0)], first_grouped[which], 0, D)
+        bias_cols = psum.tile([P, P], BF16, tag="misc")
+        nc.tensor.transpose(bias_cols[:], bias_rows[:], identity_bf[:])
+        nc.scalar.mul(out=neg_bk[:], in_=bias_cols[:, 0:n_bias_rows], mul=-score_scale)
+        nc.scalar.copy(out=bq_cols[:], in_=bias_cols[:, n_bias_rows : 2 * n_bias_rows])
+        nc.scalar.copy(out=bv0_cols[:], in_=bias_cols[:, 2 * n_bias_rows : n_stage_rows])
+        spread = psum.tile([P, D], F32, tag="misc")
+        for r in range(J_TILES):
+            nc.tensor.matmul(
+                out=spread[:, r * P : (r + 1) * P],
+                lhsT=bv0_cols[:, r : r + 1].to_broadcast([P, P]),
+                rhs=identity_bf[:],
+                start=True,
+                stop=True,
+            )
+        nc.scalar.copy(out=bv_all[:, 0:D], in_=spread[:])
+        new_grouped(0)
+        regroup(nc.vector.tensor_copy, 0, BLOCK_COL["v"], D)
+        quantise(*weight_job(0, BLOCK_COL["v"], D))
+        regroup(nc.vector.tensor_copy, 0, BLOCK_COL["k"], HALF_D)
         quantise(*x_job(0))
-        for which in ("v", "k"):
-            quantise(*weight_job(first_grouped[which], which, 0))
+        quantise(*weight_job(0, BLOCK_COL["k"], HALF_D))
+        head0_rest = [BLOCK_COL["k"] + HALF_D, BLOCK_COL["q"], BLOCK_COL["q"] + HALF_D]
 
-        for period in range(-1, N_TILES + 4):
-            project_q(period - 3)
+        for period in range(-1, last_period):
+            project_q(period - SUM_LAG + 1)
             project_k_and_v(period + 1)
             add_biases(period)
             multiply_scores(period)
-            if period == 0:
-                first_grouped["q"] = new_grouped()
-                regroup(nc.vector.tensor_copy, raw_blocks[("q", 0)], first_grouped["q"], 0, D)
-                to_quantise[period + 1].append(weight_job(first_grouped["q"], "q", 0))
+            if 0 <= period < len(head0_rest):
+                regroup(nc.vector.tensor_copy, 0, head0_rest[period], HALF_D)
+                to_quantise[period].append(weight_job(0, head0_rest[period], HALF_D))
+            if period == 1:
                 transpose_x(1)
                 to_quantise[period + 1].append(x_job(1))
+            regroup_next_head(period)
+            row_maximum(period - MAX_LAG)
+            exponentials(period - EXP_LAG)
+            weighted_sum(period - SUM_LAG)
             if period >= 0:
-                for n in range(PIECES_PER_PERIOD):
-                    regroup_stream_piece(period * PIECES_PER_PERIOD + n, period)
-            row_maximum(period - 2)
-            exponentials(period - 3)
-            weighted_sum(period - 4)
-            for job in to_quantise[period]:
-                quantise(*job)
+                for job in to_quantise[period]:
+                    quantise(*job)
 
         nc.vector.reciprocal(out=reciprocal[:], in_=denominator[:])
         nc.vector.tensor_tensor(out=result[:, 0:N_TILES], in0=numerator[:], in1=reciprocal[:], op=ALU.mult)
-        nc.vector.tensor_tensor(
-            out=result[:, 0:N_TILES].rearrange("p (b r) -> p b r", b=B),
-            in0=result[:, 0:N_TILES].rearrange("p (b r) -> p b r", b=B),
-            in1=bq_cols[:].unsqueeze(1).to_broadcast([P, B, n_bias_rows]),
-            op=ALU.add,
-        )
         turned_result = psum.tile([P, P], F32, tag="misc")
         nc.tensor.transpose(turned_result[:], result[:], identity[:])
         nc.scalar.copy(out=result_rows[:], in_=turned_result[0:N_TILES, :])

@@ -30,7 +30,6 @@ HALF_D = D // 2
 
 RUN = 4
 STEP_COLS = HEAD_COLS // TILES_PER_HEAD
-PIECE_COLS = 64
 
 MAX_LAG = 2
 EXP_LAG = 3
@@ -166,13 +165,16 @@ def tile_multihead_attention_pa_kernel(tc, x, Wq, bq, Wk, bk, Wv, bv, out):
             grouped[head] = group_pool.tile([P, HEAD_COLS, PACK], BF16, name="grouped", align_bytes=64)
 
         def regroup(copy, head, first_col, n_cols):
-            block, first_in_block = divmod(first_col, D)
-            copy(
-                out=grouped[head][:, first_col : first_col + n_cols, :].rearrange("p (c i) t -> p c t i", i=RUN),
-                in_=raw[(BLOCKS[block], head)][:, :, first_in_block : first_in_block + n_cols].rearrange(
-                    "p t (c i) -> p c t i", i=RUN
-                ),
-            )
+            for block, which in enumerate(BLOCKS):
+                lo = max(first_col, block * D)
+                hi = min(first_col + n_cols, (block + 1) * D)
+                if lo < hi:
+                    copy(
+                        out=grouped[head][:, lo:hi, :].rearrange("p (c i) t -> p c t i", i=RUN),
+                        in_=raw[(which, head)][:, :, lo - block * D : hi - block * D].rearrange(
+                            "p t (c i) -> p c t i", i=RUN
+                        ),
+                    )
 
         last_period = N_TILES + SUM_LAG
         to_quantise = {n: [] for n in range(last_period)}
@@ -184,8 +186,7 @@ def tile_multihead_attention_pa_kernel(tc, x, Wq, bq, Wk, bk, Wv, bv, out):
             head += 1
             if step == 0:
                 new_grouped(head)
-            for first_col in range(step * STEP_COLS, (step + 1) * STEP_COLS, PIECE_COLS):
-                regroup(nc.scalar.copy, head, first_col, PIECE_COLS)
+            regroup(nc.scalar.copy, head, step * STEP_COLS, STEP_COLS)
             for first_col, n_cols in ((BLOCK_COL["k"], 2 * D), (BLOCK_COL["q"], D)):
                 if step * STEP_COLS < first_col + n_cols <= (step + 1) * STEP_COLS:
                     to_quantise[period + 1].append(weight_job(head, first_col, n_cols))
@@ -238,7 +239,7 @@ def tile_multihead_attention_pa_kernel(tc, x, Wq, bq, Wk, bk, Wv, bv, out):
                 return
             project_features("q", t)
 
-        def add_biases(t):
+        def finish_k(t):
             if not 0 <= t < N_TILES:
                 return
             head, batch, j_tile = place(t)
@@ -251,16 +252,17 @@ def tile_multihead_attention_pa_kernel(tc, x, Wq, bq, Wk, bk, Wv, bv, out):
                 bias=neg_bk[:, bias_col : bias_col + 1],
                 scale=-score_scale,
             )
+            live[("neg_k", t)] = neg_k
+
+        def finish_v_and_multiply(t):
+            if not 0 <= t < N_TILES:
+                return
+            head, batch, j_tile = place(t)
             v_full = work.tile([P, S], F32, name="v_full")
             nc.vector.tensor_tensor(
                 out=v_full[:], in0=live[("v", t)][:], in1=bv_all[:, head * D : (head + 1) * D], op=ALU.add
             )
-            live[("neg_k", t)] = neg_k
             live[("v_full", t)] = v_full
-
-        def multiply_scores(t):
-            if not 0 <= t < N_TILES:
-                return
             neg_score = work.tile([P, S], F32, name="neg_score", bufs=EXP_LAG + 2)
             nc.gpsimd.tensor_tensor(out=neg_score[:], in0=live[("neg_k", t)][:], in1=live[("v_full", t)][:], op=ALU.mult)
             live[("neg_score", t)] = neg_score
@@ -329,10 +331,12 @@ def tile_multihead_attention_pa_kernel(tc, x, Wq, bq, Wk, bk, Wv, bv, out):
         head0_rest = [BLOCK_COL["k"] + HALF_D, BLOCK_COL["q"], BLOCK_COL["q"] + HALF_D]
 
         for period in range(-1, last_period):
+            bias_last = period >= 0 and len(to_quantise[period]) > 0
             project_q(period - SUM_LAG + 1)
             project_k_and_v(period + 1)
-            add_biases(period)
-            multiply_scores(period)
+            finish_k(period)
+            if not bias_last:
+                finish_v_and_multiply(period)
             if 0 <= period < len(head0_rest):
                 regroup(nc.vector.tensor_copy, 0, head0_rest[period], HALF_D)
                 to_quantise[period].append(weight_job(0, head0_rest[period], HALF_D))
@@ -346,6 +350,8 @@ def tile_multihead_attention_pa_kernel(tc, x, Wq, bq, Wk, bk, Wv, bv, out):
             if period >= 0:
                 for job in to_quantise[period]:
                     quantise(*job)
+            if bias_last:
+                finish_v_and_multiply(period)
 
         nc.vector.reciprocal(out=reciprocal[:], in_=denominator[:])
         nc.vector.tensor_tensor(out=result[:, 0:N_TILES], in0=numerator[:], in1=reciprocal[:], op=ALU.mult)

@@ -30,6 +30,7 @@ HALF_D = D // 2
 
 RUN = 4
 STEP_COLS = HEAD_COLS // TILES_PER_HEAD
+SCALAR_COLS = 2 * STEP_COLS // 3
 
 MAX_LAG = 2
 EXP_LAG = 3
@@ -179,6 +180,9 @@ def tile_multihead_attention_pa_kernel(tc, x, Wq, bq, Wk, bk, Wv, bv, out):
         last_period = N_TILES + SUM_LAG
         to_quantise = {n: [] for n in range(last_period)}
 
+        def gpsimd_copy(out, in_):
+            nc.gpsimd.tensor_scalar(out=out, in0=in_, scalar1=1.0, scalar2=0.0, op0=ALU.mult, op1=ALU.add)
+
         def regroup_next_head(period):
             if not 0 <= period < (H - 1) * TILES_PER_HEAD:
                 return
@@ -186,7 +190,8 @@ def tile_multihead_attention_pa_kernel(tc, x, Wq, bq, Wk, bk, Wv, bv, out):
             head += 1
             if step == 0:
                 new_grouped(head)
-            regroup(nc.scalar.copy, head, step * STEP_COLS, STEP_COLS)
+            regroup(nc.scalar.copy, head, step * STEP_COLS, SCALAR_COLS)
+            regroup(gpsimd_copy, head, step * STEP_COLS + SCALAR_COLS, STEP_COLS - SCALAR_COLS)
             for first_col, n_cols in ((BLOCK_COL["k"], 2 * D), (BLOCK_COL["q"], D)):
                 if step * STEP_COLS < first_col + n_cols <= (step + 1) * STEP_COLS:
                     to_quantise[period + 1].append(weight_job(head, first_col, n_cols))
@@ -335,6 +340,7 @@ def tile_multihead_attention_pa_kernel(tc, x, Wq, bq, Wk, bk, Wv, bv, out):
             project_q(period - SUM_LAG + 1)
             project_k_and_v(period + 1)
             finish_k(period)
+            regroup_next_head(period)
             if not bias_last:
                 finish_v_and_multiply(period)
             if 0 <= period < len(head0_rest):
@@ -343,7 +349,6 @@ def tile_multihead_attention_pa_kernel(tc, x, Wq, bq, Wk, bk, Wv, bv, out):
             if period == 1:
                 transpose_x(1)
                 to_quantise[period + 1].append(x_job(1))
-            regroup_next_head(period)
             row_maximum(period - MAX_LAG)
             exponentials(period - EXP_LAG)
             weighted_sum(period - SUM_LAG)

from contextlib import ExitStack
import math

import concourse.masks as masks
import concourse.mybir as mybir

BF16 = mybir.dt.bfloat16
F32 = mybir.dt.float32
U32 = mybir.dt.uint32
U8 = mybir.dt.uint8
FP8X4 = mybir.dt.float8_e4m3fn_x4
ALU = mybir.AluOpType
ACT = mybir.ActivationFunctionType

P = 128
PACK = 4
B, S, E, H, D = 2, 512, 512, 4, 512
assert E == P * PACK and S == D

J_TILES = D // P
TILES_PER_HEAD = B * J_TILES
N_TILES = H * TILES_PER_HEAD
TOKEN_TILES = S // P
HALF_E = E // 2

BLOCKS = ("k", "v", "q")
BLOCK_COL = {"k": 0, "v": D, "q": 2 * D}
HEAD_COLS = 3 * D
HALF_D = D // 2

RUN = 4
STEP_COLS = HEAD_COLS // TILES_PER_HEAD
SCALAR_COLS = 2 * STEP_COLS // 3

MAX_LAG = 2
EXP_LAG = 3
SUM_LAG = 4

FLOPS = 2 * B * S * E * 3 * H * D


def tile_multihead_attention_pa_kernel(tc, x, Wq, bq, Wk, bk, Wv, bv, out):
    nc = tc.nc
    weights = {"q": Wq, "k": Wk, "v": Wv}
    score_scale = 1.0 / math.sqrt(D)
    n_bias_rows = H * J_TILES

    with ExitStack() as ctx:
        keep = ctx.enter_context(tc.tile_pool(name="keep", bufs=1))
        group_pool = ctx.enter_context(tc.tile_pool(name="group", bufs=2))
        work = ctx.enter_context(tc.tile_pool(name="work", bufs=3))
        psum = ctx.enter_context(tc.psum_pool(name="psum", bufs=2))
        ctx.enter_context(tc.manual_schedule())

        x_raw = keep.tile([P, B * TOKEN_TILES * E], BF16)
        x_grouped = keep.tile([P, B * S * PACK], BF16, align_bytes=64)
        x_codes = keep.tile([P, B * S], U32, align_bytes=64)
        x_scales = keep.tile([P, B * S], U8, align_bytes=64)
        raw = {}
        codes = {}
        scales = {}
        grouped = {}
        for head in range(H):
            for which in BLOCKS:
                raw[(which, head)] = keep.tile([P, PACK, D], BF16, name="raw_%s%d" % (which, head))
            codes[head] = keep.tile([P, HEAD_COLS], U32, name="codes%d" % head, align_bytes=64)
            scales[head] = keep.tile([P, HEAD_COLS], U8, name="scales%d" % head, align_bytes=64)

        identity = keep.tile([P, P], F32)
        identity_bf = keep.tile([P, P], BF16)
        n_stage_rows = 2 * n_bias_rows + J_TILES
        bias_rows = keep.tile([P, P], BF16)
        neg_bk = keep.tile([P, n_bias_rows], F32)
        bq_cols = keep.tile([P, n_bias_rows], F32)
        bv0_cols = keep.tile([P, J_TILES], BF16)
        bv_all = keep.tile([P, H * D], BF16)
        zero_col = keep.tile([P, 1], F32)
        table_warm = keep.tile([P, 1], F32)
        neg_max = keep.tile([P, N_TILES], F32)
        denominator = keep.tile([P, N_TILES], F32)
        numerator = keep.tile([P, N_TILES], F32)
        reciprocal = keep.tile([P, N_TILES], F32)
        result = keep.tile([P, P], F32)
        result_rows = keep.tile([N_TILES, P], F32)
        products = keep.tile([P, S], F32)

        def load_x(batch):
            first = batch * TOKEN_TILES * E
            nc.sync.dma_start(
                out=x_raw[:, first : first + TOKEN_TILES * E].rearrange("p (n e) -> p n e", e=E),
                in_=x[batch].rearrange("(n p) e -> p n e", p=P),
            )

        def load_weight_block(which, head):
            for half in range(2):
                rows = weights[which][half * HALF_E : (half + 1) * HALF_E, head * D : (head + 1) * D]
                nc.sync.dma_start(
                    out=raw[(which, head)][:, 2 * half : 2 * half + 2, :],
                    in_=rows.rearrange("(p e) c -> p e c", e=2),
                )

        def load_bv(head):
            cols = slice(head * D, (head + 1) * D)
            nc.sync.dma_start(out=bv_all[:, cols], in_=bv[cols].partition_broadcast(P))

        load_weight_block("v", 0)
        load_x(0)
        load_weight_block("k", 0)
        load_weight_block("q", 0)
        load_weight_block("k", 1)
        load_x(1)
        load_weight_block("v", 1)
        load_weight_block("q", 1)
        load_bv(1)
        for head in range(2, H):
            for which in ("k", "v", "q"):
                load_weight_block(which, head)
            load_bv(head)

        nc.vector.memset(bias_rows[:], 0.0)
        nc.scalar.dma_start(out=bias_rows[0:n_bias_rows, :], in_=bk.rearrange("(r p) -> r p", p=P))
        nc.scalar.dma_start(out=bias_rows[n_bias_rows : 2 * n_bias_rows, :], in_=bq.rearrange("(r p) -> r p", p=P))
        nc.scalar.dma_start(out=bias_rows[2 * n_bias_rows : n_stage_rows, :], in_=bv[0:D].rearrange("(r p) -> r p", p=P))

        masks.make_identity(nc, identity[:])
        nc.vector.memset(zero_col[:], 0.0)
        nc.vector.memset(result[:], 0.0)
        nc.vector.tensor_copy(out=identity_bf[:], in_=identity[:])
        nc.scalar.activation(out=table_warm[:], in_=zero_col[:], func=ACT.Exp)

        def quantise(in_, codes_out, scales_out):
            nc.vector.quantize_mx(out=codes_out.bitcast(FP8X4), scales=scales_out, in_=in_)

        def x_job(batch):
            return (
                x_grouped[:, batch * S * PACK : (batch + 1) * S * PACK],
                x_codes[:, batch * S : (batch + 1) * S],
                x_scales[:, batch * S : (batch + 1) * S],
            )

        def weight_job(head, first_col, n_cols):
            cols = slice(first_col, first_col + n_cols)
            return (grouped[head][:, cols, :].rearrange("p c t -> p (c t)"), codes[head][:, cols], scales[head][:, cols])

        def transpose_x(batch):
            x_words = x_raw[:].bitcast(F32)
            grouped_words = x_grouped[:].bitcast(F32)
            for pair in range(TOKEN_TILES // 2):
                turned = psum.tile([P, 2, 2 * P], F32, tag="misc")
                for block in range(2):
                    n = batch * TOKEN_TILES + 2 * pair + block
                    for half in range(2):
                        first = n * (E // 2) + half * P
                        nc.tensor.transpose(
                            turned[:, half, block * P : (block + 1) * P], x_words[:, first : first + P], identity[:]
                        )
                first_token = batch * S + pair * 2 * P
                nc.scalar.copy(
                    out=grouped_words[:, 2 * first_token : 2 * (first_token + 2 * P)].rearrange(
                        "p (r u) -> p r u", u=2
                    ),
                    in_=turned[:].rearrange("p u r -> p r u"),
                )

        def new_grouped(head):
            grouped[head] = group_pool.tile([P, HEAD_COLS, PACK], BF16, name="grouped", align_bytes=64)

        def regroup(copy, head, first_col, n_cols):
            for block, which in enumerate(BLOCKS):
                lo = max(first_col, block * D)
                hi = min(first_col + n_cols, (block + 1) * D)
                if lo < hi:
                    copy(
                        out=grouped[head][:, lo:hi, :].rearrange("p (c i) t -> p c t i", i=RUN),
                        in_=raw[(which, head)][:, :, lo - block * D : hi - block * D].rearrange(
                            "p t (c i) -> p c t i", i=RUN
                        ),
                    )

        last_period = N_TILES + SUM_LAG
        to_quantise = {n: [] for n in range(last_period)}

        def gpsimd_copy(out, in_):
            nc.gpsimd.tensor_scalar(out=out, in0=in_, scalar1=1.0, scalar2=0.0, op0=ALU.mult, op1=ALU.add)

        def regroup_next_head(period):
            if not 0 <= period < (H - 1) * TILES_PER_HEAD:
                return
            head, step = divmod(period, TILES_PER_HEAD)
            head += 1
            if step == 0:
                new_grouped(head)
            regroup(nc.scalar.copy, head, step * STEP_COLS, SCALAR_COLS)
            regroup(gpsimd_copy, head, step * STEP_COLS + SCALAR_COLS, STEP_COLS - SCALAR_COLS)
            for first_col, n_cols in ((BLOCK_COL["k"], 2 * D), (BLOCK_COL["q"], D)):
                if step * STEP_COLS < first_col + n_cols <= (step + 1) * STEP_COLS:
                    to_quantise[period + 1].append(weight_job(head, first_col, n_cols))

        live = {}

        def place(t):
            head, rest = divmod(t, TILES_PER_HEAD)
            batch, j_tile = divmod(rest, J_TILES)
            return head, batch, j_tile

        def out_row(t):
            head, batch, j_tile = place(t)
            return (batch * H + head) * J_TILES + j_tile

        def project(name, t, stationary, stationary_cols, moving, moving_cols):
            bank = psum.tile([P, S], F32, name=name + "_ps", tag=name)
            nc.tensor.matmul_mx(
                out=bank[:],
                lhsT=stationary[0][:, stationary_cols].bitcast(FP8X4),
                lhsT_scale=stationary[1][:, stationary_cols],
                rhs=moving[0][:, moving_cols].bitcast(FP8X4),
                rhs_scale=moving[1][:, moving_cols],
                start=True,
                stop=True,
            )
            live[(name, t)] = bank

        def project_features(name, t):
            head, batch, j_tile = place(t)
            first = BLOCK_COL[name] + j_tile * P
            project(
                name, t, (codes[head], scales[head]), slice(first, first + P),
                (x_codes, x_scales), slice(batch * S, (batch + 1) * S),
            )

        def project_k_and_v(t):
            if not 0 <= t < N_TILES:
                return
            head, batch, j_tile = place(t)
            project_features("k", t)
            first = batch * S + j_tile * P
            project(
                "v", t, (x_codes, x_scales), slice(first, first + P),
                (codes[head], scales[head]), slice(BLOCK_COL["v"], BLOCK_COL["v"] + D),
            )

        def project_q(t):
            if not 0 <= t < N_TILES:
                return
            project_features("q", t)

        def finish_k(t):
            if not 0 <= t < N_TILES:
                return
            head, batch, j_tile = place(t)
            bias_col = head * J_TILES + j_tile
            neg_k = work.tile([P, S], F32, name="neg_k")
            nc.scalar.activation(
                out=neg_k[:],
                in_=live[("k", t)][:],
                func=ACT.Identity,
                bias=neg_bk[:, bias_col : bias_col + 1],
                scale=-score_scale,
            )
            live[("neg_k", t)] = neg_k

        def finish_v_and_multiply(t):
            if not 0 <= t < N_TILES:
                return
            head, batch, j_tile = place(t)
            v_full = work.tile([P, S], F32, name="v_full")
            nc.vector.tensor_tensor(
                out=v_full[:], in0=live[("v", t)][:], in1=bv_all[:, head * D : (head + 1) * D], op=ALU.add
            )
            live[("v_full", t)] = v_full
            neg_score = work.tile([P, S], F32, name="neg_score", bufs=EXP_LAG + 2)
            nc.gpsimd.tensor_tensor(out=neg_score[:], in0=live[("neg_k", t)][:], in1=live[("v_full", t)][:], op=ALU.mult)
            live[("neg_score", t)] = neg_score

        def row_maximum(t):
            if not 0 <= t < N_TILES:
                return
            col = out_row(t)
            nc.vector.tensor_reduce(
                out=neg_max[:, col : col + 1], in_=live[("neg_score", t)][:], axis=mybir.AxisListType.X, op=ALU.min
            )

        def exponentials(t):
            if not 0 <= t < N_TILES:
                return
            col = out_row(t)
            weight = work.tile([P, S], F32, name="weight")
            nc.scalar.activation(
                out=weight[:],
                in_=live[("neg_score", t)][:],
                func=ACT.Exp,
                bias=neg_max[:, col : col + 1],
                scale=-1.0,
                accum_out=denominator[:, col : col + 1],
            )
            live[("weight", t)] = weight

        def weighted_sum(t):
            if not 0 <= t < N_TILES:
                return
            head, batch, j_tile = place(t)
            bias_col = head * J_TILES + j_tile
            col = out_row(t)
            nc.vector.scalar_tensor_tensor(
                out=products[:],
                in0=live[("q", t)][:],
                scalar=bq_cols[:, bias_col : bias_col + 1],
                in1=live[("weight", t)][:],
                op0=ALU.add,
                op1=ALU.mult,
                accum_out=numerator[:, col : col + 1],
            )

        transpose_x(0)
        bias_cols = psum.tile([P, P], BF16, tag="misc")
        nc.tensor.transpose(bias_cols[:], bias_rows[:], identity_bf[:])
        nc.scalar.mul(out=neg_bk[:], in_=bias_cols[:, 0:n_bias_rows], mul=-score_scale)
        nc.scalar.copy(out=bq_cols[:], in_=bias_cols[:, n_bias_rows : 2 * n_bias_rows])
        nc.scalar.copy(out=bv0_cols[:], in_=bias_cols[:, 2 * n_bias_rows : n_stage_rows])
        spread = psum.tile([P, D], F32, tag="misc")
        for r in range(J_TILES):
            nc.tensor.matmul(
                out=spread[:, r * P : (r + 1) * P],
                lhsT=bv0_cols[:, r : r + 1].to_broadcast([P, P]),
                rhs=identity_bf[:],
                start=True,
                stop=True,
            )
        nc.scalar.copy(out=bv_all[:, 0:D], in_=spread[:])
        new_grouped(0)
        regroup(nc.vector.tensor_copy, 0, BLOCK_COL["v"], D)
        quantise(*weight_job(0, BLOCK_COL["v"], D))
        regroup(nc.vector.tensor_copy, 0, BLOCK_COL["k"], HALF_D)
        quantise(*x_job(0))
        quantise(*weight_job(0, BLOCK_COL["k"], HALF_D))
        head0_rest = [BLOCK_COL["k"] + HALF_D, BLOCK_COL["q"], BLOCK_COL["q"] + HALF_D]

        for period in range(-1, last_period):
            bias_last = period >= 0 and len(to_quantise[period]) > 0
            project_q(period - SUM_LAG + 1)
            project_k_and_v(period + 1)
            finish_k(period)
            regroup_next_head(period)
            if not bias_last:
                finish_v_and_multiply(period)
            if 0 <= period < len(head0_rest):
                regroup(nc.vector.tensor_copy, 0, head0_rest[period], HALF_D)
                to_quantise[period].append(weight_job(0, head0_rest[period], HALF_D))
            if period == 1:
                transpose_x(1)
                to_quantise[period + 1].append(x_job(1))
            row_maximum(period - MAX_LAG)
            exponentials(period - EXP_LAG)
            weighted_sum(period - SUM_LAG)
            if period >= 0:
                for job in to_quantise[period]:
                    quantise(*job)
            if bias_last:
                finish_v_and_multiply(period)

        nc.vector.reciprocal(out=reciprocal[:], in_=denominator[:])
        nc.vector.tensor_tensor(out=result[:, 0:N_TILES], in0=numerator[:], in1=reciprocal[:], op=ALU.mult)
        turned_result = psum.tile([P, P], F32, tag="misc")
        nc.tensor.transpose(turned_result[:], result[:], identity[:])
        nc.scalar.copy(out=result_rows[:], in_=turned_result[0:N_TILES, :])
        nc.sync.dma_start(out=out.rearrange("b h (n p) -> (b h n) p", p=P), in_=result_rows[:])
